import numpy as np
import ml_dtypes


def mxq(x, axis, fmt="e4m3"):
    dtype, down = {"e4m3": (ml_dtypes.float8_e4m3fn, 7), "e5m2": (ml_dtypes.float8_e5m2, 14)}[fmt]
    v = np.moveaxis(np.asarray(x, np.float32).astype(ml_dtypes.bfloat16).astype(np.float64), axis, -1)
    blocks = v.reshape(v.shape[:-1] + (-1, 32))
    amax = np.abs(blocks).max(-1, keepdims=True)
    byte = np.maximum(np.where(amax > 0, np.frexp(amax)[1] - 1 + 127, 0) - down, 1)
    scale = np.exp2(byte - 127.0)
    codes = (blocks / scale).astype(np.float32).astype(dtype).astype(np.float64)
    return np.moveaxis((codes * scale).reshape(v.shape), -1, axis)


WIDE = False


def mx_kscale(k):
    if not WIDE:
        return np.ones(k)
    levels = np.array([18, -18])
    if k % 512:
        return np.exp2(np.random.permutation(np.resize(levels, k // 32))).repeat(32)
    a = np.empty((k // 512, 16))
    for p in range(k // 512):
        a[p, :8] = np.random.permutation(np.resize(levels, 8))
        for g in range(8):
            far = levels[np.abs(levels - a[p, g]) >= 10]
            a[p, g + 8] = far[np.random.randint(len(far))]
    return np.exp2(a.ravel()).repeat(32)


BF16 = ml_dtypes.bfloat16


def bf(x):
    return np.asarray(x, np.float32).astype(BF16)


def f64(x):
    return np.asarray(x).astype(np.float64)


B, E, D1, D2, WS1, WS2, H = 2, 1024, 32, 16, 8, 8, 32
NW = (D1 // WS1) * (D2 // WS2)
S = WS1 * WS2
DH = E // H
T = B * NW * S


def to_image(v):
    c = v.shape[-1]
    v = v.reshape(B, D1 // WS1, D2 // WS2, WS1, WS2, c).transpose(0, 1, 3, 2, 4, 5).reshape(B, D1, D2, c)
    return np.roll(v, (WS1 // 2, WS2 // 2), axis=(1, 2))


def to_windows(g):
    c = g.shape[-1]
    g = np.roll(g, (-(WS1 // 2), -(WS2 // 2)), axis=(1, 2))
    return g.reshape(B, D1 // WS1, WS1, D2 // WS2, WS2, c).transpose(0, 1, 3, 2, 4, 5).reshape(T, c)


def setup_inputs():
    n = np.random.standard_normal
    s = mx_kscale(T)
    u = mx_kscale(E)
    z0 = bf(n((B, NW, H, S, DH)) * 0.4)
    x = bf(n((B, E, D1, D2)))
    w0 = bf(n((E, E)) / np.sqrt(E))
    bo = bf(0.1 * n(E))
    g = n((B, D1, D2, E)) * np.exp2(np.random.randint(-6, 1, (B, D1, D2, 1))) * 4.0
    return {"z_heads": bf(f64(z0) * s.reshape(B, NW, 1, S, 1)),
            "x": x,
            "Wo": bf(f64(w0) / u),
            "bo": bo,
            "grad_out": bf(g / to_image(s.reshape(T, 1)) * u)}


def reference(z_heads, x, Wo, bo, grad_out):
    dp = to_windows(f64(grad_out))
    z = f64(z_heads).transpose(0, 1, 3, 2, 4).reshape(T, E)
    dz = mxq(dp, 1, "e5m2") @ mxq(f64(Wo), 1, "e4m3").T
    dw = mxq(z, 0, "e4m3").T @ mxq(dp, 0, "e5m2")
    dz_heads = dz.reshape(B, NW, S, H, DH).transpose(0, 1, 3, 2, 4)
    return dz_heads, dw

from contextlib import ExitStack

import concourse.mybir as mybir
from concourse.masks import make_identity

F32 = mybir.dt.float32
BF16 = mybir.dt.bfloat16
U32 = mybir.dt.uint32
U8 = mybir.dt.uint8
E4M3 = mybir.dt.float8_e4m3fn_x4
E5M2 = mybir.dt.float8_e5m2_x4

P = 128
E = 1024
FLOPS = 2 * 2 * E * E * E
BYTES = 3 * 2 * E * E + 2 * 4 * E * E


def tile_functatransformer_pb_v_kernel(tc, z_heads, x, Wo, bo, grad_out, out_0, out_1):
    nc = tc.nc
    with ExitStack() as ctx:
        keep = ctx.enter_context(tc.tile_pool(name="keep", bufs=1))
        psum = ctx.enter_context(tc.psum_pool(name="psum", bufs=4))
        ctx.enter_context(tc.manual_schedule())

        wo_raw = [keep.tile([P, 2, E], BF16, name=f"wo_raw{c}", align_bytes=64) for c in range(4)]
        dp_raw = [keep.tile([P, 4, E], BF16, name=f"dp_raw{w}", align_bytes=64) for w in range(2)]
        z_raw = [keep.tile([P, 32, 128], BF16, name=f"z_raw{w}", align_bytes=64) for w in range(2)]
        ident = keep.tile([P, P], F32, name="ident", align_bytes=64)
        perm = keep.tile([P, P], F32, name="perm", align_bytes=64)
        zperm = keep.tile([P, P], BF16, name="zperm", align_bytes=64)
        wo_g = [[keep.tile([P, 512 * 4], BF16, name=f"wo_g{g}{n}", align_bytes=64) for n in range(2)] for g in range(2)]
        wo_c = [[keep.tile([P, 512], U32, name=f"wo_c{g}{n}", align_bytes=64) for n in range(2)] for g in range(2)]
        wo_s = [[keep.tile([P, 512], U8, name=f"wo_s{g}{n}", align_bytes=64) for n in range(2)] for g in range(2)]
        df_g = [[keep.tile([P, 512 * 4], BF16, name=f"df_g{g}{n}", align_bytes=64) for n in range(2)] for g in range(2)]
        df_c = [[keep.tile([P, 512], U32, name=f"df_c{g}{n}", align_bytes=64) for n in range(2)] for g in range(2)]
        df_s = [[keep.tile([P, 512], U8, name=f"df_s{g}{n}", align_bytes=64) for n in range(2)] for g in range(2)]
        dt_g = [[keep.tile([P, 512 * 4], BF16, name=f"dt_g{w}{n}", align_bytes=64) for n in range(2)] for w in range(2)]
        dt_c = [[keep.tile([P, 512], U32, name=f"dt_c{w}{n}", align_bytes=64) for n in range(2)] for w in range(2)]
        dt_s = [[keep.tile([P, 512], U8, name=f"dt_s{w}{n}", align_bytes=64) for n in range(2)] for w in range(2)]
        z_g = [[keep.tile([P, 512 * 4], BF16, name=f"z_g{w}{n}", align_bytes=64) for n in range(2)] for w in range(2)]
        z_c = [[keep.tile([P, 512], U32, name=f"z_c{w}{n}", align_bytes=64) for n in range(2)] for w in range(2)]
        z_s = [[keep.tile([P, 512], U8, name=f"z_s{w}{n}", align_bytes=64) for n in range(2)] for w in range(2)]
        st0 = [keep.tile([P, 16, 8, 32], F32, name=f"st0_{n}", align_bytes=64) for n in range(2)]
        st1 = [keep.tile([P, E], F32, name=f"st1_{m % 4}", align_bytes=64) for m in range(8)]

        def load_wo(c):
            nc.sync.dma_start(out=wo_raw[c][:], in_=Wo[256 * c : 256 * c + 256, :].rearrange("(n p) e -> p n e", p=P))

        def load_dp(w):
            rows = grad_out.rearrange("b i (q j) e -> (b i) q j e", j=4)
            for hf in range(2):
                q = (2 * w + hf + 1) % 4
                nc.sync.dma_start(out=dp_raw[w][hf:P:2, :, :], in_=rows[:, q, :, :])

        def load_z(w, bw):
            b, wr = divmod(bw, 4)
            nc.sync.dma_start(
                out=z_raw[w][bw:P:8, :, :],
                in_=z_heads[b, 2 * wr + w].rearrange("h (q j) d -> q h (j d)", j=4),
            )

        copy_on = {"s": nc.scalar.copy, "v": nc.vector.tensor_copy}

        def wo_transposes(c, g, eng):
            bank = psum.tile([P, 2, 256], F32, name="tr")
            for n in range(2):
                words = wo_raw[c][:, n, :].bitcast(F32)
                for u in range(2):
                    nc.tensor.transpose(bank[:, u, 128 * n : 128 * n + 128], words[:, 256 * g + u : 256 * g + 256 : 2], ident[:])
            half, r = divmod(c, 2)
            dst = wo_g[g][half][:].bitcast(F32).rearrange("p (c u) -> p c u", u=2)[:, 256 * r : 256 * r + 256, :]
            copy_on[eng](out=dst, in_=bank[:].rearrange("p u c -> p c u"))

        def dp_transposes(w, jp, g, eng):
            bank = psum.tile([P, 2, 256], F32, name="tr")
            for jj in range(2):
                words = dp_raw[w][:, 2 * jp + jj, :].bitcast(F32)
                for u in range(2):
                    nc.tensor.transpose(bank[:, u, 128 * jj : 128 * jj + 128], words[:, 256 * g + u : 256 * g + 256 : 2], perm[:])
            dst = df_g[g][jp][:].bitcast(F32).rearrange("p (x w c u) -> p x w c u", w=2, c=8, u=2)[:, :, w, :, :]
            copy_on[eng](out=dst, in_=bank[:].rearrange("p u (x c) -> p x c u", c=8))

        def quant(codes, scales, src, fmt):
            nc.vector.quantize_mx(out=codes[:].bitcast(fmt), scales=scales[:], in_=src[:])

        def out0_tile(jp, t, half, eng):
            acc = psum.tile([P, 512], F32, name="mm")
            for g in range(2):
                nc.tensor.matmul_mx(
                    out=acc[:],
                    lhsT=df_c[g][jp][:, 128 * t : 128 * t + 128].bitcast(E5M2),
                    lhsT_scale=df_s[g][jp][:, 128 * t : 128 * t + 128],
                    rhs=wo_c[g][half][:].bitcast(E4M3),
                    rhs_scale=wo_s[g][half][:],
                    start=(g == 0),
                    stop=(g == 1),
                )
            jj, hf = divmod(t, 2)
            s8 = 4 * hf + 2 * jp + jj
            copy_on[eng](out=st0[half][:, :, s8, :], in_=acc[:].rearrange("p (h d) -> p h d", d=32))

        def store0(half):
            for h in range(16):
                view = out_0[:, :, 16 * half + h].rearrange("b w (s i) d -> (b w) s (i d)", i=8)
                src = st0[half][:, h, :, :].rearrange("p i d -> p (i d)")
                nc.sync.dma_start(out=view, in_=src)

        def dt_interleave(w, n, k):
            c0 = 512 * n + 256 * k
            nc.vector.tensor_copy(
                out=dt_g[w][n][:, 1024 * k : 1024 * k + 1024].rearrange("p (e j) -> p e j", j=4),
                in_=dp_raw[w][:, :, c0 : c0 + 256].rearrange("p j e -> p e j"),
            )

        def z_chunk(w, k, eng):
            bank = psum.tile([P, 2, 512], BF16, name="tr")
            for i in range(2):
                h0 = 8 * k + 4 * i
                nc.tensor.matmul(
                    bank[:, i, :], zperm[:], z_raw[w][:, h0 : h0 + 4, :].rearrange("p h x -> p (h x)"), start=True, stop=True
                )
            n, r = divmod(k, 2)
            copy_on[eng](
                out=z_g[w][n][:, 1024 * r : 1024 * r + 1024].rearrange("p (h d j) -> p h d j", h=8, j=4),
                in_=bank[:].rearrange("p i (h j d) -> p (i h) d j", j=4, d=32),
            )

        def out1_tile(m, n, eng):
            acc = psum.tile([P, 512], F32, name="mm")
            nh, r = divmod(m, 4)
            for w in range(2):
                nc.tensor.matmul_mx(
                    out=acc[:],
                    lhsT=z_c[w][nh][:, 128 * r : 128 * r + 128].bitcast(E4M3),
                    lhsT_scale=z_s[w][nh][:, 128 * r : 128 * r + 128],
                    rhs=dt_c[w][n][:].bitcast(E5M2),
                    rhs_scale=dt_s[w][n][:],
                    start=(w == 0),
                    stop=(w == 1),
                )
            copy_on[eng](out=st1[m][:, 512 * n : 512 * n + 512], in_=acc[:])

        load_wo(0)
        load_wo(1)
        load_dp(0)
        load_dp(1)
        load_wo(2)
        load_wo(3)
        for w in range(2):
            for bw in range(4):
                load_z(w, bw)
                load_z(w, bw + 4)
        make_identity(nc, ident[:])
        pv = perm[:].rearrange("p (hf b wr sh sl) -> p hf b wr sh sl", hf=2, b=2, wr=4, sh=2)
        iv = ident[:].rearrange("p (b k m sl hf) -> p hf b k m sl", b=2, k=4, m=2, sl=4)
        zv = zperm[:].rearrange("p (b k m sq) -> p b k m sq", b=2, k=4, m=2)
        jv = ident[:].rearrange("p (sh sq b wr) -> p b wr sh sq", sh=2, sq=8, b=2)
        for b in range(2):
            nc.vector.tensor_copy(out=pv[:, :, b, :, 0, :], in_=iv[:, :, b, :, 1, :])
            nc.vector.tensor_copy(out=pv[:, :, b, 0:3, 1, :], in_=iv[:, :, b, 1:4, 0, :])
            nc.vector.tensor_copy(out=pv[:, :, b, 3, 1, :], in_=iv[:, :, b, 0, 0, :])
        for b in range(2):
            nc.vector.tensor_copy(out=zv[:, b, :, 1, :], in_=jv[:, b, :, 0, :])
            nc.vector.tensor_copy(out=zv[:, b, 1:4, 0, :], in_=jv[:, b, 0:3, 1, :])
            nc.vector.tensor_copy(out=zv[:, b, 0, 0, :], in_=jv[:, b, 3, 1, :])

        for c in range(2):
            wo_transposes(c, 0, "s")
            wo_transposes(c, 1, "v")
        quant(wo_c[0][0], wo_s[0][0], wo_g[0][0], E4M3)
        quant(wo_c[1][0], wo_s[1][0], wo_g[1][0], E4M3)
        dp_transposes(0, 0, 0, "s")
        dp_transposes(0, 0, 1, "v")
        dp_transposes(0, 1, 0, "s")
        dp_transposes(0, 1, 1, "s")
        dt_interleave(0, 0, 0)
        dt_interleave(0, 0, 1)
        dp_transposes(1, 0, 0, "s")
        dp_transposes(1, 0, 1, "v")
        dp_transposes(1, 1, 0, "s")
        dp_transposes(1, 1, 1, "v")
        quant(df_c[0][0], df_s[0][0], df_g[0][0], E5M2)
        quant(df_c[1][0], df_s[1][0], df_g[1][0], E5M2)
        wo_transposes(2, 0, "s")
        wo_transposes(2, 1, "s")
        quant(df_c[0][1], df_s[0][1], df_g[0][1], E5M2)
        quant(df_c[1][1], df_s[1][1], df_g[1][1], E5M2)
        wo_transposes(3, 0, "s")
        wo_transposes(3, 1, "v")
        for jp in range(2):
            for t in range(4):
                out0_tile(jp, t, 0, "s")
        store0(0)
        dt_interleave(0, 1, 0)
        quant(wo_c[0][1], wo_s[0][1], wo_g[0][1], E4M3)
        quant(wo_c[1][1], wo_s[1][1], wo_g[1][1], E4M3)
        dt_interleave(0, 1, 1)
        dt_interleave(1, 0, 0)
        dt_interleave(1, 0, 1)
        dt_interleave(1, 1, 0)
        dt_interleave(1, 1, 1)
        for jp in range(2):
            for t in range(4):
                out0_tile(jp, t, 1, "s")
        store0(1)
        for w in range(2):
            for n in range(2):
                quant(dt_c[w][n], dt_s[w][n], dt_g[w][n], E5M2)
        z_chunk(0, 0, "v")
        z_chunk(0, 1, "v")
        z_chunk(0, 2, "v")
        z_chunk(0, 3, "s")
        z_chunk(1, 0, "v")
        z_chunk(1, 1, "s")
        quant(z_c[0][0], z_s[0][0], z_g[0][0], E4M3)
        quant(z_c[1][0], z_s[1][0], z_g[1][0], E4M3)
        z_chunk(1, 2, "v")
        z_chunk(1, 3, "s")
        for m in range(4):
            out1_tile(m, 0, "s")
            out1_tile(m, 1, "v")
            nc.sync.dma_start(out=out_1[128 * m : 128 * m + 128, :], in_=st1[m][:])
            if m == 0:
                quant(z_c[0][1], z_s[0][1], z_g[0][1], E4M3)
                quant(z_c[1][1], z_s[1][1], z_g[1][1], E4M3)
        for m in range(4, 8):
            out1_tile(m, 0, "s")
            out1_tile(m, 1, "v")
            nc.sync.dma_start(out=out_1[128 * m : 128 * m + 128, :], in_=st1[m][:])
